import numpy as np
import ml_dtypes


def mxq(x, axis, fmt="e4m3"):
    dtype, down = {"e4m3": (ml_dtypes.float8_e4m3fn, 7), "e5m2": (ml_dtypes.float8_e5m2, 14)}[fmt]
    v = np.moveaxis(np.asarray(x, np.float32).astype(ml_dtypes.bfloat16).astype(np.float64), axis, -1)
    blocks = v.reshape(v.shape[:-1] + (-1, 32))
    amax = np.abs(blocks).max(-1, keepdims=True)
    byte = np.maximum(np.where(amax > 0, np.frexp(amax)[1] - 1 + 127, 0) - down, 1)
    scale = np.exp2(byte - 127.0)
    codes = (blocks / scale).astype(np.float32).astype(dtype).astype(np.float64)
    return np.moveaxis((codes * scale).reshape(v.shape), -1, axis)


WIDE = False


def mx_kscale(k):
    if not WIDE:
        return np.ones(k)
    levels = np.array([10, -10, 5, -5, 0])
    a = np.random.permutation(np.resize(levels, k // 512 * 4)).reshape(k // 512, 4)
    idx = np.arange(k)
    return np.exp2(a[idx // 512, idx % 128 // 32])


BF16 = ml_dtypes.bfloat16


def bf(x):
    return np.asarray(x, np.float32).astype(BF16)


def f64(x):
    return np.asarray(x).astype(np.float64)


E2M1 = np.array([0.0, 0.5, 1.0, 1.5, 2.0, 3.0, 4.0, 6.0, -0.0, -0.5, -1.0, -1.5, -2.0, -3.0, -4.0, -6.0])


def pack_weight(w, fmt):
    k, n = w.shape
    w = f64(bf(w)).reshape(k // 32, 32, n)
    amax = np.abs(w).max(1)
    if fmt == "e4m3":
        byte = np.frexp(amax)[1] - 1 + 127 - 7
    else:
        mant, ex = np.frexp(amax / 6.0)
        byte = np.where(mant > 0.5, ex, ex - 1) + 127
    byte = np.clip(np.where(amax > 0, byte, 1), 1, 254)
    scaled = (w * np.exp2(127.0 - byte)[:, None, :]).reshape(k, n).astype(np.float32)
    by_word = np.ascontiguousarray(scaled.reshape(k // 512, 128, 4, n).transpose(0, 1, 3, 2))
    if fmt == "e4m3":
        words = by_word.astype(ml_dtypes.float8_e4m3fn).view(np.uint8)
    else:
        c = by_word.astype(ml_dtypes.float4_e2m1fn).view(np.uint8) & 0xF
        words = c[..., 0::2] | (c[..., 1::2] << 4)
    return np.ascontiguousarray(words), np.ascontiguousarray(byte.astype(np.uint8).reshape(k // 512, 16, n))


def unpack_weight(words, scales, fmt):
    g, p, n, _ = words.shape
    if fmt == "e4m3":
        vals = np.ascontiguousarray(words).view(ml_dtypes.float8_e4m3fn).astype(np.float64)
    else:
        nib = np.empty((g, p, n, 4), np.uint8)
        nib[..., 0::2] = words & 0xF
        nib[..., 1::2] = words >> 4
        vals = E2M1[nib]
    vals = vals * np.repeat(np.exp2(scales.astype(np.float64) - 127.0), 8, axis=1)[..., None]
    return vals.transpose(0, 1, 3, 2).reshape(g * 512, n)


B, DI, H = 128, 2048, 2048
EPS = 1e-5
FMT = "e4m3"


def _ln(v):
    m = np.mean(v, axis=-1, keepdims=True)
    var = np.var(v, axis=-1, keepdims=True)
    return (v - m) / np.sqrt(var + EPS)


def sigmoid(v):
    return 1.0 / (1.0 + np.exp(-v))


def setup_inputs():
    s = mx_kscale(DI)
    x = bf(np.random.standard_normal((B, DI)) * s)
    hx = bf(np.random.standard_normal((B, H)))
    w_i2h = np.random.standard_normal((3 * H, DI)) / np.sqrt(DI) / s[None, :]
    b_i2h = bf(np.random.standard_normal(3 * H) * 0.3)
    w_h2h = np.random.standard_normal((3 * H, H)) / np.sqrt(H)
    b_h2h = bf(np.random.standard_normal(3 * H) * 0.3)
    i_words, i_scales = pack_weight(np.ascontiguousarray(w_i2h.T), FMT)
    h_words, h_scales = pack_weight(np.ascontiguousarray(w_h2h.T), FMT)
    return {"x": x,
            "hx": hx,
            "W_i2h_words": i_words,
            "W_i2h_scales": i_scales,
            "b_i2h": b_i2h,
            "W_h2h_words": h_words,
            "W_h2h_scales": h_scales,
            "b_h2h": b_h2h}


def reference(x, hx, W_i2h_words, W_i2h_scales, b_i2h, W_h2h_words, W_h2h_scales, b_h2h):
    hx = f64(hx)
    xt = (mxq(f64(x), 1, "e4m3") @ unpack_weight(W_i2h_words, W_i2h_scales, FMT)) + f64(b_i2h)
    ht = (mxq(hx, 1, "e4m3") @ unpack_weight(W_h2h_words, W_h2h_scales, FMT)) + f64(b_h2h)
    x_new = xt[:, 2 * H:]
    h_new = ht[:, 2 * H:]
    gates = sigmoid(_ln(xt[:, : 2 * H]) + _ln(ht[:, : 2 * H]))
    r_t = gates[:, :H]
    z_t = gates[:, H:]
    n_t = np.tanh(_ln(x_new) + r_t * _ln(h_new))
    h_t = z_t * hx + (1.0 - z_t) * n_t
    return h_t

@@ -1,0 +1,412 @@
+from contextlib import ExitStack
+
+import concourse.mybir as mybir
+from concourse.masks import make_identity
+
+F32 = mybir.dt.float32
+BF16 = mybir.dt.bfloat16
+I32 = mybir.dt.int32
+U8 = mybir.dt.uint8
+U32 = mybir.dt.uint32
+FP8X4 = mybir.dt.float8_e4m3fn_x4
+ALU = mybir.AluOpType
+ACT = mybir.ActivationFunctionType
+AX = mybir.AxisListType
+
+P = 128
+DI = 2048
+H = 2048
+NOUT = 3 * H
+KG = DI // 512
+CH = 512
+BLK = 2048
+EPS = 1e-5
+
+FLOPS = 2 * 2 * P * DI * NOUT
+
+
+def tile_layernormgrucell_w_kernel(
+    tc, x, hx, wi_words, wi_scales, b_i, wh_words, wh_scales, b_h, out
+):
+    nc = tc.nc
+    with ExitStack() as ctx:
+        ctx.enter_context(tc.manual_schedule())
+        const = ctx.enter_context(tc.tile_pool(name="const", bufs=1))
+        small = ctx.enter_context(tc.tile_pool(name="small", bufs=1))
+        wpool = ctx.enter_context(tc.tile_pool(name="wpool", bufs=11))
+        junkp = ctx.enter_context(tc.tile_pool(name="junkp", bufs=2))
+        psum = ctx.enter_context(tc.psum_pool(name="psum", bufs=8))
+
+        def col(name, width=1):
+            return small.tile([P, width], F32, name=name)
+
+        brows = const.tile([P, CH], BF16, name="brows")
+        nc.vector.memset(brows[:], 0.0)
+        warm = col("warm")
+        nc.vector.memset(warm[:], 0.0)
+        planes_i = const.tile([P, NOUT], U8, name="planes_i", align_bytes=64)
+        planes_h = const.tile([P, NOUT], U8, name="planes_h", align_bytes=64)
+        nc.vector.memset(planes_i[:].bitcast(I32), 0)
+        nc.vector.memset(planes_h[:].bitcast(I32), 0)
+        mhalf = col("mhalf")
+        nc.vector.memset(mhalf[:], -0.5)
+        ident_f = const.tile([P, P], F32, name="ident_f")
+        make_identity(nc, ident_f[:])
+        ident_b = const.tile([P, P], BF16, name="ident_b")
+        make_identity(nc, ident_b[:])
+
+        x_sb = const.tile([P, DI], BF16, name="x_sb", align_bytes=64)
+        hx_sb = const.tile([P, H], BF16, name="hx_sb", align_bytes=64)
+        nc.sync.dma_start(out=x_sb[:], in_=x[:, :])
+        nc.sync.dma_start(out=hx_sb[:], in_=hx[:, :])
+        nc.scalar.dma_start(out=brows[0:12, :], in_=b_i.rearrange("(r c) -> r c", c=CH))
+        nc.scalar.dma_start(out=brows[12:24, :], in_=b_h.rearrange("(r c) -> r c", c=CH))
+        warm2 = col("warm2")
+        nc.scalar.activation(out=warm2[:], in_=warm[:], func=ACT.Sigmoid)
+        for planes, scales in ((planes_i, wi_scales), (planes_h, wh_scales)):
+            for q in range(4):
+                nc.sync.dma_start(
+                    out=planes[32 * q : 32 * q + 16, :].bitcast(I32),
+                    in_=scales[:, 4 * q : 4 * q + 4, :].bitcast(I32),
+                )
+
+        ops = []
+        for nm, src in (("x", x_sb), ("h", hx_sb)):
+            words = src[:].bitcast(F32)
+            grouped = const.tile([P, DI], BF16, name="grouped_" + nm, align_bytes=64)
+            gw = grouped[:].bitcast(F32)
+            for hf in range(2):
+                tp = psum.tile([P, 4, P], F32, tag="bank", name="tp_%s%d" % (nm, hf))
+                for gg in range(2):
+                    g = 2 * hf + gg
+                    for u in range(2):
+                        nc.tensor.transpose(
+                            tp[:, 2 * gg + u, :],
+                            words[:, 256 * g + u : 256 * (g + 1) : 2],
+                            ident_f[:],
+                        )
+                dst = gw[:, 512 * hf : 512 * (hf + 1)].rearrange(
+                    "p (g b u) -> p g b u", g=2, u=2
+                )
+                srcv = tp[:].rearrange("p (g u) b -> p g b u", g=2)
+                if hf == 0:
+                    nc.vector.tensor_copy(out=dst, in_=srcv)
+                else:
+                    nc.scalar.copy(out=dst, in_=srcv)
+            codes = const.tile([P, KG * P], U32, name="codes_" + nm, align_bytes=64)
+            cscale = const.tile([P, KG * P], U8, name="cscale_" + nm, align_bytes=64)
+            ops.append((grouped, codes, cscale))
+        for grouped, codes, cscale in ops:
+            nc.vector.quantize_mx(
+                out=codes[:].bitcast(FP8X4), scales=cscale[:], in_=grouped[:]
+            )
+        op_x = (ops[0][1], ops[0][2])
+        op_h = (ops[1][1], ops[1][2])
+
+        bias_sb = const.tile([P, 2 * NOUT], BF16, name="bias_sb")
+        for i in range(12):
+            bp = psum.tile([P, 2 * CH], BF16, tag="bank", name="bp%d" % i)
+            for hf in range(2):
+                j = 2 * i + hf
+                nc.tensor.matmul(
+                    out=bp[:, CH * hf : CH * (hf + 1)],
+                    lhsT=ident_b[:, j : j + 1].to_broadcast([P, P]),
+                    rhs=brows[:],
+                    start=True,
+                    stop=True,
+                )
+            nc.scalar.copy(out=bias_sb[:, 2 * CH * i : 2 * CH * (i + 1)], in_=bp[:])
+
+        def load_g(name, words, g, c0, ncols):
+            wt = wpool.tile([P, 4 * ncols], U8, tag="w", name=name, align_bytes=64)
+            nc.sync.dma_start(
+                out=wt[:].bitcast(I32),
+                in_=words[g, :, c0 : c0 + ncols, :]
+                .rearrange("p n t -> p (n t)")
+                .bitcast(I32),
+            )
+            return wt
+
+        def load_gs(name, words, g0, ng, c0, ncols):
+            wt = wpool.tile([P, ng, 4 * ncols], U8, tag="w", name=name, align_bytes=64)
+            nc.sync.dma_start(
+                out=wt[:].bitcast(I32),
+                in_=words[g0 : g0 + ng, :, c0 : c0 + ncols, :]
+                .rearrange("g p n t -> p g (n t)")
+                .bitcast(I32),
+            )
+            return wt
+
+        def mx_pass(acc, op, g, rhs, planes, pcol, n):
+            codes, cscale = op
+            nc.tensor.matmul_mx(
+                out=acc[:, 0:n],
+                lhsT=codes[:, P * g : P * (g + 1)].bitcast(FP8X4),
+                lhsT_scale=cscale[:, P * g : P * (g + 1)],
+                rhs=rhs.bitcast(FP8X4),
+                rhs_scale=planes[4 * g : P, pcol : pcol + n],
+                start=(g == 0),
+                stop=(g == KG - 1),
+            )
+
+        def bank(name):
+            return psum.tile([P, CH], F32, tag="bank", name=name)
+
+        def make_group(name, nsum, nsq, ncols):
+            return {
+                "name": name,
+                "inv_n": 1.0 / ncols,
+                "nsq": nsq,
+                "sums": col(name + "_sums", nsum),
+                "sq": col(name + "_sq", nsq),
+                "negc": col(name + "_negc"),
+            }
+
+        def evac(grp, k, acc, ys, bcol, n):
+            nc.vector.scalar_tensor_tensor(
+                out=ys,
+                in0=acc[:, 0:n],
+                scalar=1.0,
+                in1=bias_sb[:, bcol : bcol + n],
+                op0=ALU.mult,
+                op1=ALU.add,
+                accum_out=grp["sums"][:, k : k + 1],
+            )
+            if k == 0:
+                nc.vector.tensor_scalar_mul(
+                    out=grp["negc"][:], in0=grp["sums"][:, 0:1], scalar1=-1.0 / n
+                )
+
+        def square(grp, k, ys, n):
+            junk = junkp.tile([P, 2 * CH], F32, tag="junk", name="junk_%s%d" % (grp["name"], k))
+            nc.scalar.activation(
+                out=junk[:, 0:n],
+                in_=ys,
+                func=ACT.Square,
+                bias=grp["negc"][:, 0:1],
+                scale=1.0,
+                accum_out=grp["sq"][:, k : k + 1],
+            )
+
+        def stats_pre(grp):
+            nm = grp["name"]
+            tot = col(nm + "_tot")
+            dm = col(nm + "_dm")
+            grp["dm2e"] = col(nm + "_dm2e")
+            grp["negmean"] = col(nm + "_negmean")
+            grp["s2p"] = col(nm + "_s2p")
+            nc.vector.reduce_sum(out=tot[:], in_=grp["sums"][:], axis=AX.X)
+            nc.vector.tensor_scalar(
+                out=dm[:], in0=tot[:], scalar1=grp["inv_n"], scalar2=grp["negc"][:, 0:1],
+                op0=ALU.mult, op1=ALU.add,
+            )
+            nc.vector.tensor_tensor(
+                out=grp["negmean"][:], in0=grp["negc"][:], in1=dm[:], op=ALU.subtract
+            )
+            nc.vector.tensor_scalar(
+                out=grp["dm2e"][:], in0=dm[:], scalar1=dm[:, 0:1], scalar2=EPS,
+                op0=ALU.mult, op1=ALU.subtract,
+            )
+
+        def stats_s2p(grp):
+            nc.vector.reduce_sum(
+                out=grp["s2p"][:], in_=grp["sq"][:, 0 : grp["nsq"] - 1], axis=AX.X
+            )
+
+        def stats_post(grp, times=None):
+            nm = grp["name"]
+            last = grp["nsq"] - 1
+            ms = col(nm + "_ms")
+            veps = col(nm + "_veps")
+            nc.vector.tensor_scalar(
+                out=ms[:], in0=grp["sq"][:, last : last + 1],
+                scalar1=grp["s2p"][:, 0:1], scalar2=grp["inv_n"],
+                op0=ALU.add, op1=ALU.mult,
+            )
+            if times is None:
+                nc.vector.tensor_scalar_sub(
+                    out=veps[:], in0=ms[:], scalar1=grp["dm2e"][:, 0:1]
+                )
+            else:
+                nc.vector.tensor_scalar(
+                    out=veps[:], in0=ms[:],
+                    scalar1=grp["dm2e"][:, 0:1], scalar2=times[:, 0:1],
+                    op0=ALU.subtract, op1=ALU.mult,
+                )
+            return veps
+
+        def rsqrt(name, v):
+            r = col(name)
+            nc.gpsimd.tensor_tensor(out=r[:], in0=v[:], in1=mhalf[:], op=ALU.pow)
+            return r
+
+        def run_block(name, words, planes, op, wcol0, grp, c0, y, boff, split):
+            accs = [bank("%s_%d" % (name, j)) for j in range(BLK // CH)]
+            for g in range(KG - 1):
+                wt = load_g("w_%s_%d" % (name, g), words, g, wcol0, BLK)
+                for j in range(BLK // CH):
+                    mx_pass(accs[j], op, g, wt[:, 4 * CH * j : 4 * CH * (j + 1)],
+                            planes, wcol0 + CH * j, CH)
+            g = KG - 1
+            per = BLK // split
+            for s in range(split):
+                wt = load_g("w_%s_%d_%d" % (name, g, s), words, g, wcol0 + per * s, per)
+                for jj in range(per // CH):
+                    j = s * (per // CH) + jj
+                    mx_pass(accs[j], op, g, wt[:, 4 * CH * jj : 4 * CH * (jj + 1)],
+                            planes, wcol0 + CH * j, CH)
+            for pr in range(2):
+                for jj in range(2):
+                    c = c0 + 2 * pr + jj
+                    evac(grp, c, accs[2 * pr + jj], y[:, CH * c : CH * (c + 1)],
+                         boff + CH * c, CH)
+                c = c0 + 2 * pr
+                square(grp, c // 2, y[:, CH * c : CH * (c + 2)], 2 * CH)
+
+        yxg = const.tile([P, 2 * H], F32, name="yxg")
+        yhg = const.tile([P, 2 * H], F32, name="yhg")
+        yhn = const.tile([P, H], F32, name="yhn")
+        yxn = const.tile([P, H], F32, name="yxn")
+        omz = const.tile([P, H], F32, name="omz")
+        zh = const.tile([P, H], F32, name="zh")
+        g_xg = make_group("xg", 8, 4, 2 * H)
+        g_hg = make_group("hg", 8, 4, 2 * H)
+        g_hn = make_group("hn", 4, 2, H)
+        g_xn = make_group("xn", 5, 5, H)
+
+        run_block("xg0", wi_words, planes_i, op_x, 0, g_xg, 0, yxg, 0, 1)
+        run_block("xg1", wi_words, planes_i, op_x, BLK, g_xg, 4, yxg, 0, 1)
+        stats_pre(g_xg)
+        stats_s2p(g_xg)
+        rstd_xg = rsqrt("xg_rstd", stats_post(g_xg))
+        nb_xg = col("xg_nb")
+        nc.vector.tensor_tensor(
+            out=nb_xg[:], in0=g_xg["negmean"][:], in1=rstd_xg[:], op=ALU.mult
+        )
+        for hf in range(2):
+            sl = yxg[:, H * hf : H * (hf + 1)]
+            nc.scalar.activation(
+                out=sl, in_=sl, func=ACT.Identity,
+                bias=nb_xg[:, 0:1], scale=rstd_xg[:, 0:1],
+            )
+
+        run_block("hg0", wh_words, planes_h, op_h, 0, g_hg, 0, yhg, NOUT, 1)
+        run_block("hg1", wh_words, planes_h, op_h, BLK, g_hg, 4, yhg, NOUT, 2)
+        stats_pre(g_hg)
+        stats_s2p(g_hg)
+        rstd_hg = rsqrt("hg_rstd", stats_post(g_hg))
+        nb_hg = col("hg_nb")
+        nc.vector.tensor_tensor(
+            out=nb_hg[:], in0=g_hg["negmean"][:], in1=rstd_hg[:], op=ALU.mult
+        )
+
+        acc_hn = [bank("hn_%d" % j) for j in range(4)]
+        for g in range(KG):
+            wt = load_g("w_hn_%d" % g, wh_words, g, 2 * H, BLK)
+            for j in range(4):
+                mx_pass(acc_hn[j], op_h, g, wt[:, 4 * CH * j : 4 * CH * (j + 1)],
+                        planes_h, 2 * H + CH * j, CH)
+
+        for pc in range(4):
+            sl = yhg[:, 1024 * pc : 1024 * (pc + 1)]
+            nc.vector.scalar_tensor_tensor(
+                out=sl, in0=sl, scalar=rstd_hg[:, 0:1],
+                in1=yxg[:, 1024 * pc : 1024 * (pc + 1)],
+                op0=ALU.mult, op1=ALU.add,
+            )
+            nc.scalar.activation(
+                out=sl, in_=sl, func=ACT.Sigmoid, bias=nb_hg[:, 0:1], scale=1.0
+            )
+            if pc >= 2:
+                cs = slice(1024 * (pc - 2), 1024 * (pc - 1))
+                nc.gpsimd.tensor_scalar(
+                    out=omz[:, cs], in0=sl, scalar1=-1.0, scalar2=1.0,
+                    op0=ALU.mult, op1=ALU.add,
+                )
+                nc.gpsimd.tensor_tensor(
+                    out=zh[:, cs], in0=sl, in1=hx_sb[:, cs], op=ALU.mult
+                )
+
+        for pr in range(2):
+            for jj in range(2):
+                c = 2 * pr + jj
+                evac(g_hn, c, acc_hn[c], yhn[:, CH * c : CH * (c + 1)],
+                     NOUT + 2 * H + CH * c, CH)
+            square(g_hn, pr, yhn[:, 2 * CH * pr : 2 * CH * (pr + 1)], 2 * CH)
+        stats_pre(g_hn)
+        qn = const.tile([P, H], F32, name="qn")
+        for pc in range(2):
+            cs = slice(1024 * pc, 1024 * (pc + 1))
+            nc.vector.scalar_tensor_tensor(
+                out=qn[:, cs], in0=yhn[:, cs], scalar=g_hn["negmean"][:, 0:1],
+                in1=yhg[:, cs], op0=ALU.add, op1=ALU.mult,
+            )
+
+        chunks = ((0, 512), (512, 512), (1024, 512), (1536, 256), (1792, 256))
+        acc_xn = [bank("xn_%d" % k) for k in range(5)]
+        for hf in range(2):
+            wt = load_gs("w_xn_a%d" % hf, wi_words, 2 * hf, 2, 2 * H, 2 * CH)
+            for k in range(2):
+                for gg in range(2):
+                    mx_pass(acc_xn[k], op_x, 2 * hf + gg,
+                            wt[:, gg, 4 * CH * k : 4 * CH * (k + 1)],
+                            planes_i, 2 * H + CH * k, CH)
+        for k in range(5):
+            cc, n = chunks[k]
+            if k >= 2:
+                wt = load_gs("w_xn_%d" % k, wi_words, 0, KG, 2 * H + cc, n)
+                for g in range(KG):
+                    mx_pass(acc_xn[k], op_x, g, wt[:, g, :], planes_i, 2 * H + cc, n)
+            evac(g_xn, k, acc_xn[k], yxn[:, cc : cc + n], 2 * H + cc, n)
+            square(g_xn, k, yxn[:, cc : cc + n], n)
+            if k == 1:
+                stats_s2p(g_hn)
+                veps_hn = stats_post(g_hn)
+                rstd_hn = rsqrt("hn_rstd", veps_hn)
+                inv_hn = col("hn_inv")
+                nc.vector.reciprocal(out=inv_hn[:], in_=veps_hn[:])
+        stats_pre(g_xn)
+        stats_s2p(g_xn)
+        rho = rsqrt("xn_rho", stats_post(g_xn, times=inv_hn))
+        nb = col("xn_nb")
+
+        def p1(j):
+            cc, n = chunks[j]
+            nc.vector.scalar_tensor_tensor(
+                out=yxn[:, cc : cc + n], in0=yxn[:, cc : cc + n], scalar=rho[:, 0:1],
+                in1=qn[:, cc : cc + n], op0=ALU.mult, op1=ALU.add,
+            )
+
+        def p2(j):
+            cc, n = chunks[j]
+            nc.scalar.activation(
+                out=yxn[:, cc : cc + n], in_=yxn[:, cc : cc + n], func=ACT.Tanh,
+                bias=nb[:, 0:1], scale=rstd_hn[:, 0:1],
+            )
+
+        def p3(j):
+            cc, n = chunks[j]
+            sl = yxn[:, cc : cc + n]
+            nc.vector.tensor_tensor(out=sl, in0=sl, in1=omz[:, cc : cc + n], op=ALU.mult)
+            nc.vector.tensor_tensor(out=sl, in0=sl, in1=zh[:, cc : cc + n], op=ALU.add)
+            nc.sync.dma_start(out=out[:, cc : cc + n], in_=sl)
+
+        p1(0)
+        nc.vector.tensor_scalar(
+            out=nb[:], in0=g_xn["negmean"][:], scalar1=rho[:, 0:1], scalar2=rstd_hn[:, 0:1],
+            op0=ALU.mult, op1=ALU.mult,
+        )
+        p2(0)
+        p1(1)
+        p2(1)
+        p1(2)
+        p2(2)
+        p3(0)
+        p1(3)
+        p2(3)
+        p1(4)
+        p2(4)
+        p3(1)
+        p3(2)
+        p3(3)
+        p3(4)

@@ -63,12 +63,22 @@ def tile_layernormgrucell_w_kernel(
         nc.scalar.dma_start(out=brows[12:24, :], in_=b_h.rearrange("(r c) -> r c", c=CH))
         warm2 = col("warm2")
         nc.scalar.activation(out=warm2[:], in_=warm[:], func=ACT.Sigmoid)
-        for planes, scales in ((planes_i, wi_scales), (planes_h, wh_scales)):
-            for q in range(4):
-                nc.sync.dma_start(
-                    out=planes[32 * q : 32 * q + 16, :].bitcast(I32),
-                    in_=scales[:, 4 * q : 4 * q + 4, :].bitcast(I32),
-                )
+        for q in range(4):
+            nc.sync.dma_start(
+                out=planes_i[32 * q : 32 * q + 16, 0 : 2 * H].bitcast(I32),
+                in_=wi_scales[:, 4 * q : 4 * q + 4, 0 : 2 * H].bitcast(I32),
+            )
+
+        def scale_rows_gpsimd(planes, scales, c0, c1):
+            for r in range(4):
+                for q in (0, 2, 1, 3):
+                    p0 = 32 * q + r
+                    nc.gpsimd.dma_start(
+                        out=planes[p0 : p0 + 13 : 4, c0:c1].bitcast(F32),
+                        in_=scales[:, 4 * q + r, c0:c1].bitcast(F32),
+                    )
+
+        scale_rows_gpsimd(planes_h, wh_scales, 0, NOUT)
 
         ops = []
         for nm, src in (("x", x_sb), ("h", hx_sb)):
@@ -279,6 +289,7 @@ def tile_layernormgrucell_w_kernel(
         stats_pre(g_xg)
         stats_s2p(g_xg)
         rstd_xg = rsqrt("xg_rstd", stats_post(g_xg))
+        scale_rows_gpsimd(planes_i, wi_scales, 2 * H, NOUT)
         nb_xg = col("xg_nb")
         nc.vector.tensor_tensor(
             out=nb_xg[:], in0=g_xg["negmean"][:], in1=rstd_xg[:], op=ALU.mult

@@ -48,7 +48,7 @@ def tile_layernormgrucell_w_kernel(
         planes_h = const.tile([P, NOUT], U8, name="planes_h", align_bytes=64)
         nc.vector.memset(planes_i[:].bitcast(I32), 0)
         nc.vector.memset(planes_h[:].bitcast(I32), 0)
-        mhalf = col("mhalf")
+        mhalf = col("mhalf", 2)
         nc.vector.memset(mhalf[:], -0.5)
         ident_f = const.tile([P, P], F32, name="ident_f")
         make_identity(nc, ident_f[:])
@@ -63,22 +63,12 @@ def tile_layernormgrucell_w_kernel(
         nc.scalar.dma_start(out=brows[12:24, :], in_=b_h.rearrange("(r c) -> r c", c=CH))
         warm2 = col("warm2")
         nc.scalar.activation(out=warm2[:], in_=warm[:], func=ACT.Sigmoid)
-        for q in range(4):
-            nc.sync.dma_start(
-                out=planes_i[32 * q : 32 * q + 16, 0 : 2 * H].bitcast(I32),
-                in_=wi_scales[:, 4 * q : 4 * q + 4, 0 : 2 * H].bitcast(I32),
-            )
-
-        def scale_rows_gpsimd(planes, scales, c0, c1):
-            for r in range(4):
-                for q in (0, 2, 1, 3):
-                    p0 = 32 * q + r
-                    nc.gpsimd.dma_start(
-                        out=planes[p0 : p0 + 13 : 4, c0:c1].bitcast(F32),
-                        in_=scales[:, 4 * q + r, c0:c1].bitcast(F32),
-                    )
-
-        scale_rows_gpsimd(planes_h, wh_scales, 0, NOUT)
+        for planes, scales in ((planes_i, wi_scales), (planes_h, wh_scales)):
+            for q in range(4):
+                nc.sync.dma_start(
+                    out=planes[32 * q : 32 * q + 16, :].bitcast(I32),
+                    in_=scales[:, 4 * q : 4 * q + 4, :].bitcast(I32),
+                )
 
         ops = []
         for nm, src in (("x", x_sb), ("h", hx_sb)):
@@ -165,11 +155,18 @@ def tile_layernormgrucell_w_kernel(
         def make_group(name, nsum, nsq, ncols):
             return {
                 "name": name,
+                "ncols": ncols,
                 "inv_n": 1.0 / ncols,
+                "nsum": nsum,
                 "nsq": nsq,
                 "sums": col(name + "_sums", nsum),
                 "sq": col(name + "_sq", nsq),
                 "negc": col(name + "_negc"),
+                "totp": col(name + "_totp"),
+                "aa": col(name + "_aa"),
+                "dm": col(name + "_dm"),
+                "negmean": col(name + "_negmean"),
+                "kk": col(name + "_kk"),
             }
 
         def evac(grp, k, acc, ys, bcol, n):
@@ -198,59 +195,63 @@ def tile_layernormgrucell_w_kernel(
                 accum_out=grp["sq"][:, k : k + 1],
             )
 
-        def stats_pre(grp):
-            nm = grp["name"]
-            tot = col(nm + "_tot")
-            dm = col(nm + "_dm")
-            grp["dm2e"] = col(nm + "_dm2e")
-            grp["negmean"] = col(nm + "_negmean")
-            grp["s2p"] = col(nm + "_s2p")
-            nc.vector.reduce_sum(out=tot[:], in_=grp["sums"][:], axis=AX.X)
+        def stats_early_sum(grp):
+            rs = col(grp["name"] + "_rs")
+            nc.vector.reduce_sum(
+                out=rs[:], in_=grp["sums"][:, 0 : grp["nsum"] - 1], axis=AX.X
+            )
             nc.vector.tensor_scalar(
-                out=dm[:], in0=tot[:], scalar1=grp["inv_n"], scalar2=grp["negc"][:, 0:1],
+                out=grp["totp"][:], in0=grp["negc"][:], scalar1=float(grp["ncols"]),
+                scalar2=rs[:, 0:1], op0=ALU.mult, op1=ALU.add,
+            )
+
+        def stats_early_sq(grp, nearly, times=None):
+            rq = col(grp["name"] + "_rq")
+            nc.vector.reduce_sum(out=rq[:], in_=grp["sq"][:, 0:nearly], axis=AX.X)
+            if times is None:
+                nc.vector.tensor_scalar(
+                    out=grp["aa"][:], in0=rq[:], scalar1=-grp["inv_n"], scalar2=EPS,
+                    op0=ALU.mult, op1=ALU.subtract,
+                )
+            else:
+                a0 = col(grp["name"] + "_a0")
+                nc.vector.tensor_scalar(
+                    out=a0[:], in0=rq[:], scalar1=-grp["inv_n"], scalar2=EPS,
+                    op0=ALU.mult, op1=ALU.subtract,
+                )
+                nc.vector.tensor_tensor(
+                    out=grp["aa"][:], in0=a0[:], in1=times[:], op=ALU.mult
+                )
+
+        def stats_dm(grp, dst, factor):
+            last = grp["nsum"] - 1
+            nc.vector.tensor_scalar(
+                out=dst, in0=grp["sums"][:, last : last + 1],
+                scalar1=grp["totp"][:, 0:1], scalar2=factor,
+                op0=ALU.add, op1=ALU.mult,
+            )
+
+        def stats_negmean(grp):
+            nc.vector.tensor_tensor(
+                out=grp["negmean"][:], in0=grp["negc"][:], in1=grp["dm"][:],
+                op=ALU.subtract,
+            )
+
+        def stats_kk(grp, d):
+            nc.vector.scalar_tensor_tensor(
+                out=grp["kk"][:], in0=d, scalar=d, in1=grp["aa"][:],
                 op0=ALU.mult, op1=ALU.add,
             )
-            nc.vector.tensor_tensor(
-                out=grp["negmean"][:], in0=grp["negc"][:], in1=dm[:], op=ALU.subtract
-            )
+
+        def stats_final(grp, dst, factor):
+            last = grp["nsq"] - 1
             nc.vector.tensor_scalar(
-                out=grp["dm2e"][:], in0=dm[:], scalar1=dm[:, 0:1], scalar2=EPS,
+                out=dst, in0=grp["sq"][:, last : last + 1],
+                scalar1=factor, scalar2=grp["kk"][:, 0:1],
                 op0=ALU.mult, op1=ALU.subtract,
             )
 
-        def stats_s2p(grp):
-            nc.vector.reduce_sum(
-                out=grp["s2p"][:], in_=grp["sq"][:, 0 : grp["nsq"] - 1], axis=AX.X
-            )
-
-        def stats_post(grp, times=None):
-            nm = grp["name"]
-            last = grp["nsq"] - 1
-            ms = col(nm + "_ms")
-            veps = col(nm + "_veps")
-            nc.vector.tensor_scalar(
-                out=ms[:], in0=grp["sq"][:, last : last + 1],
-                scalar1=grp["s2p"][:, 0:1], scalar2=grp["inv_n"],
-                op0=ALU.add, op1=ALU.mult,
-            )
-            if times is None:
-                nc.vector.tensor_scalar_sub(
-                    out=veps[:], in0=ms[:], scalar1=grp["dm2e"][:, 0:1]
-                )
-            else:
-                nc.vector.tensor_scalar(
-                    out=veps[:], in0=ms[:],
-                    scalar1=grp["dm2e"][:, 0:1], scalar2=times[:, 0:1],
-                    op0=ALU.subtract, op1=ALU.mult,
-                )
-            return veps
-
-        def rsqrt(name, v):
-            r = col(name)
-            nc.gpsimd.tensor_tensor(out=r[:], in0=v[:], in1=mhalf[:], op=ALU.pow)
-            return r
-
-        def run_block(name, words, planes, op, wcol0, grp, c0, y, boff, split):
+        def run_block(name, words, planes, op, wcol0, grp, c0, q0, y, boff, last):
             accs = [bank("%s_%d" % (name, j)) for j in range(BLK // CH)]
             for g in range(KG - 1):
                 wt = load_g("w_%s_%d" % (name, g), words, g, wcol0, BLK)
@@ -258,6 +259,7 @@ def tile_layernormgrucell_w_kernel(
                     mx_pass(accs[j], op, g, wt[:, 4 * CH * j : 4 * CH * (j + 1)],
                             planes, wcol0 + CH * j, CH)
             g = KG - 1
+            split = 2 if last else 1
             per = BLK // split
             for s in range(split):
                 wt = load_g("w_%s_%d_%d" % (name, g, s), words, g, wcol0 + per * s, per)
@@ -265,35 +267,61 @@ def tile_layernormgrucell_w_kernel(
                     j = s * (per // CH) + jj
                     mx_pass(accs[j], op, g, wt[:, 4 * CH * jj : 4 * CH * (jj + 1)],
                             planes, wcol0 + CH * j, CH)
-            for pr in range(2):
-                for jj in range(2):
-                    c = c0 + 2 * pr + jj
-                    evac(grp, c, accs[2 * pr + jj], y[:, CH * c : CH * (c + 1)],
-                         boff + CH * c, CH)
-                c = c0 + 2 * pr
-                square(grp, c // 2, y[:, CH * c : CH * (c + 2)], 2 * CH)
+
+            def ev(j):
+                c = c0 + j
+                evac(grp, c, accs[j], y[:, CH * c : CH * (c + 1)], boff + CH * c, CH)
+
+            ev(0)
+            ev(1)
+            square(grp, q0, y[:, CH * c0 : CH * (c0 + 2)], 2 * CH)
+            ev(2)
+            if not last:
+                ev(3)
+                square(grp, q0 + 1, y[:, CH * (c0 + 2) : CH * (c0 + 4)], 2 * CH)
+            else:
+                square(grp, q0 + 1, y[:, CH * (c0 + 2) : CH * (c0 + 3)], CH)
+                stats_early_sum(grp)
+                ev(3)
+                square(grp, q0 + 2, y[:, CH * (c0 + 3) : CH * (c0 + 4)], CH)
+                stats_dm(grp, grp["dm"][:], grp["inv_n"])
+                stats_early_sq(grp, grp["nsq"] - 1)
+                stats_kk(grp, grp["dm"][:, 0:1])
+                stats_negmean(grp)
 
         yxg = const.tile([P, 2 * H], F32, name="yxg")
         yhg = const.tile([P, 2 * H], F32, name="yhg")
         yhn = const.tile([P, H], F32, name="yhn")
         yxn = const.tile([P, H], F32, name="yxn")
+        qn = const.tile([P, H], F32, name="qn")
         omz = const.tile([P, H], F32, name="omz")
         zh = const.tile([P, H], F32, name="zh")
-        g_xg = make_group("xg", 8, 4, 2 * H)
-        g_hg = make_group("hg", 8, 4, 2 * H)
+        g_xg = make_group("xg", 8, 5, 2 * H)
+        g_hg = make_group("hg", 8, 5, 2 * H)
         g_hn = make_group("hn", 4, 2, H)
         g_xn = make_group("xn", 5, 5, H)
 
-        run_block("xg0", wi_words, planes_i, op_x, 0, g_xg, 0, yxg, 0, 1)
-        run_block("xg1", wi_words, planes_i, op_x, BLK, g_xg, 4, yxg, 0, 1)
-        stats_pre(g_xg)
-        stats_s2p(g_xg)
-        rstd_xg = rsqrt("xg_rstd", stats_post(g_xg))
-        scale_rows_gpsimd(planes_i, wi_scales, 2 * H, NOUT)
-        nb_xg = col("xg_nb")
-        nc.vector.tensor_tensor(
-            out=nb_xg[:], in0=g_xg["negmean"][:], in1=rstd_xg[:], op=ALU.mult
-        )
+        def gate_stats(grp):
+            nm = grp["name"]
+            veps = col(nm + "_veps")
+            rstd = col(nm + "_rstd")
+            stats_final(grp, veps[:], grp["inv_n"])
+            nc.gpsimd.tensor_tensor(
+                out=rstd[:], in0=veps[:], in1=mhalf[:, 0:1], op=ALU.pow
+            )
+            return rstd
+
+        def times_rstd(name, grp, rstd):
+            nb = col(name)
+            nc.vector.tensor_tensor(
+                out=nb[:], in0=grp["negmean"][:], in1=rstd[:], op=ALU.mult
+            )
+            return nb
+
+        run_block("xg0", wi_words, planes_i, op_x, 0, g_xg, 0, 0, yxg, 0, False)
+        run_block("xg1", wi_words, planes_i, op_x, BLK, g_xg, 4, 2, yxg, 0, True)
+        rstd_xg = gate_stats(g_xg)
+        nb_xg = times_rstd("xg_nb", g_xg, rstd_xg)
         for hf in range(2):
             sl = yxg[:, H * hf : H * (hf + 1)]
             nc.scalar.activation(
@@ -301,15 +329,9 @@ def tile_layernormgrucell_w_kernel(
                 bias=nb_xg[:, 0:1], scale=rstd_xg[:, 0:1],
             )
 
-        run_block("hg0", wh_words, planes_h, op_h, 0, g_hg, 0, yhg, NOUT, 1)
-        run_block("hg1", wh_words, planes_h, op_h, BLK, g_hg, 4, yhg, NOUT, 2)
-        stats_pre(g_hg)
-        stats_s2p(g_hg)
-        rstd_hg = rsqrt("hg_rstd", stats_post(g_hg))
-        nb_hg = col("hg_nb")
-        nc.vector.tensor_tensor(
-            out=nb_hg[:], in0=g_hg["negmean"][:], in1=rstd_hg[:], op=ALU.mult
-        )
+        run_block("hg0", wh_words, planes_h, op_h, 0, g_hg, 0, 0, yhg, NOUT, False)
+        run_block("hg1", wh_words, planes_h, op_h, BLK, g_hg, 4, 2, yhg, NOUT, True)
+        rstd_hg = gate_stats(g_hg)
 
         acc_hn = [bank("hn_%d" % j) for j in range(4)]
         for g in range(KG):
@@ -318,13 +340,16 @@ def tile_layernormgrucell_w_kernel(
                 mx_pass(acc_hn[j], op_h, g, wt[:, 4 * CH * j : 4 * CH * (j + 1)],
                         planes_h, 2 * H + CH * j, CH)
 
-        for pc in range(4):
+        nb_hg = None
+        for pc in (2, 3, 0, 1):
             sl = yhg[:, 1024 * pc : 1024 * (pc + 1)]
             nc.vector.scalar_tensor_tensor(
                 out=sl, in0=sl, scalar=rstd_hg[:, 0:1],
                 in1=yxg[:, 1024 * pc : 1024 * (pc + 1)],
                 op0=ALU.mult, op1=ALU.add,
             )
+            if nb_hg is None:
+                nb_hg = times_rstd("hg_nb", g_hg, rstd_hg)
             nc.scalar.activation(
                 out=sl, in_=sl, func=ACT.Sigmoid, bias=nb_hg[:, 0:1], scale=1.0
             )
@@ -338,14 +363,19 @@ def tile_layernormgrucell_w_kernel(
                     out=zh[:, cs], in0=sl, in1=hx_sb[:, cs], op=ALU.mult
                 )
 
-        for pr in range(2):
-            for jj in range(2):
-                c = 2 * pr + jj
-                evac(g_hn, c, acc_hn[c], yhn[:, CH * c : CH * (c + 1)],
-                     NOUT + 2 * H + CH * c, CH)
-            square(g_hn, pr, yhn[:, 2 * CH * pr : 2 * CH * (pr + 1)], 2 * CH)
-        stats_pre(g_hn)
-        qn = const.tile([P, H], F32, name="qn")
+        def ev_hn(c):
+            evac(g_hn, c, acc_hn[c], yhn[:, CH * c : CH * (c + 1)],
+                 NOUT + 2 * H + CH * c, CH)
+
+        ev_hn(0)
+        ev_hn(1)
+        square(g_hn, 0, yhn[:, 0 : 2 * CH], 2 * CH)
+        ev_hn(2)
+        stats_early_sum(g_hn)
+        ev_hn(3)
+        square(g_hn, 1, yhn[:, 2 * CH : 4 * CH], 2 * CH)
+        stats_dm(g_hn, g_hn["dm"][:], g_hn["inv_n"])
+        stats_negmean(g_hn)
         for pc in range(2):
             cs = slice(1024 * pc, 1024 * (pc + 1))
             nc.vector.scalar_tensor_tensor(
@@ -355,6 +385,15 @@ def tile_layernormgrucell_w_kernel(
 
         chunks = ((0, 512), (512, 512), (1024, 512), (1536, 256), (1792, 256))
         acc_xn = [bank("xn_%d" % k) for k in range(5)]
+        veps_hn = col("hn_veps")
+        rstd_hn = col("hn_rstd")
+        inv_hn = col("hn_inv")
+        fac_xn = col("xn_fac")
+        negfac_xn = col("xn_negfac")
+        dsc_xn = col("xn_dsc")
+        dms = col("xn_dms")
+        ratio = col("xn_ratio")
+        rho = col("xn_rho")
         for hf in range(2):
             wt = load_gs("w_xn_a%d" % hf, wi_words, 2 * hf, 2, 2 * H, 2 * CH)
             for k in range(2):
@@ -368,17 +407,40 @@ def tile_layernormgrucell_w_kernel(
                 wt = load_gs("w_xn_%d" % k, wi_words, 0, KG, 2 * H + cc, n)
                 for g in range(KG):
                     mx_pass(acc_xn[k], op_x, g, wt[:, g, :], planes_i, 2 * H + cc, n)
+            if k == 4:
+                stats_early_sum(g_xn)
             evac(g_xn, k, acc_xn[k], yxn[:, cc : cc + n], 2 * H + cc, n)
             square(g_xn, k, yxn[:, cc : cc + n], n)
             if k == 1:
-                stats_s2p(g_hn)
-                veps_hn = stats_post(g_hn)
-                rstd_hn = rsqrt("hn_rstd", veps_hn)
-                inv_hn = col("hn_inv")
+                stats_early_sq(g_hn, 1)
+                stats_kk(g_hn, g_hn["dm"][:, 0:1])
+                stats_final(g_hn, veps_hn[:], g_hn["inv_n"])
+                nc.gpsimd.tensor_tensor(
+                    out=rstd_hn[:], in0=veps_hn[:], in1=mhalf[:, 0:1], op=ALU.pow
+                )
+            if k == 2:
                 nc.vector.reciprocal(out=inv_hn[:], in_=veps_hn[:])
-        stats_pre(g_xn)
-        stats_s2p(g_xn)
-        rho = rsqrt("xn_rho", stats_post(g_xn, times=inv_hn))
+                nc.vector.tensor_scalar_mul(
+                    out=fac_xn[:], in0=inv_hn[:], scalar1=g_xn["inv_n"]
+                )
+                nc.vector.tensor_scalar_mul(
+                    out=negfac_xn[:], in0=inv_hn[:], scalar1=-g_xn["inv_n"]
+                )
+            if k == 3:
+                stats_early_sq(g_xn, 3, times=inv_hn)
+                nc.vector.tensor_scalar_mul(
+                    out=dsc_xn[:], in0=rstd_hn[:], scalar1=g_xn["inv_n"]
+                )
+        stats_dm(g_xn, dms[:], dsc_xn[:, 0:1])
+        nc.vector.scalar_tensor_tensor(
+            out=g_xn["aa"][:], in0=g_xn["sq"][:, 3:4], scalar=negfac_xn[:, 0:1],
+            in1=g_xn["aa"][:], op0=ALU.mult, op1=ALU.add,
+        )
+        stats_kk(g_xn, dms[:, 0:1])
+        stats_final(g_xn, ratio[:], fac_xn[:, 0:1])
+        nc.gpsimd.tensor_tensor(out=rho[:], in0=ratio[:], in1=mhalf[:, 0:1], op=ALU.pow)
+        stats_dm(g_xn, g_xn["dm"][:], g_xn["inv_n"])
+        stats_negmean(g_xn)
         nb = col("xn_nb")
 
         def p1(j):
@@ -399,6 +461,10 @@ def tile_layernormgrucell_w_kernel(
             cc, n = chunks[j]
             sl = yxn[:, cc : cc + n]
             nc.vector.tensor_tensor(out=sl, in0=sl, in1=omz[:, cc : cc + n], op=ALU.mult)
+
+        def p4(j):
+            cc, n = chunks[j]
+            sl = yxn[:, cc : cc + n]
             nc.vector.tensor_tensor(out=sl, in0=sl, in1=zh[:, cc : cc + n], op=ALU.add)
             nc.sync.dma_start(out=out[:, cc : cc + n], in_=sl)
 
@@ -415,9 +481,14 @@ def tile_layernormgrucell_w_kernel(
         p3(0)
         p1(3)
         p2(3)
+        p4(0)
+        p3(1)
         p1(4)
         p2(4)
-        p3(1)
+        p4(1)
         p3(2)
         p3(3)
+        p4(2)
         p3(4)
+        p4(3)
+        p4(4)

@@ -43,13 +43,11 @@ def tile_layernormgrucell_w_kernel(
         brows = const.tile([P, CH], BF16, name="brows")
         nc.vector.memset(brows[:], 0.0)
         warm = col("warm")
-        nc.vector.memset(warm[:], 0.0)
+        nc.vector.memset(warm[:], 1.0)
         planes_i = const.tile([P, NOUT], U8, name="planes_i", align_bytes=64)
         planes_h = const.tile([P, NOUT], U8, name="planes_h", align_bytes=64)
         nc.vector.memset(planes_i[:].bitcast(I32), 0)
         nc.vector.memset(planes_h[:].bitcast(I32), 0)
-        mhalf = col("mhalf", 2)
-        nc.vector.memset(mhalf[:], -0.5)
         ident_f = const.tile([P, P], F32, name="ident_f")
         make_identity(nc, ident_f[:])
         ident_b = const.tile([P, P], BF16, name="ident_b")
@@ -62,7 +60,7 @@ def tile_layernormgrucell_w_kernel(
         nc.scalar.dma_start(out=brows[0:12, :], in_=b_i.rearrange("(r c) -> r c", c=CH))
         nc.scalar.dma_start(out=brows[12:24, :], in_=b_h.rearrange("(r c) -> r c", c=CH))
         warm2 = col("warm2")
-        nc.scalar.activation(out=warm2[:], in_=warm[:], func=ACT.Sigmoid)
+        nc.scalar.activation(out=warm2[:], in_=warm[:], func=ACT.Abs_reciprocal_sqrt)
         for planes, scales in ((planes_i, wi_scales), (planes_h, wh_scales)):
             for q in range(4):
                 nc.sync.dma_start(
@@ -149,6 +147,15 @@ def tile_layernormgrucell_w_kernel(
                 stop=(g == KG - 1),
             )
 
+        def two_banks(name, accs, words, planes, op, wcol0):
+            for hf in range(2):
+                wt = load_gs("%s%d" % (name, hf), words, 2 * hf, 2, wcol0, 2 * CH)
+                for k in range(2):
+                    for gg in range(2):
+                        mx_pass(accs[k], op, 2 * hf + gg,
+                                wt[:, gg, 4 * CH * k : 4 * CH * (k + 1)],
+                                planes, wcol0 + CH * k, CH)
+
         def bank(name):
             return psum.tile([P, CH], F32, tag="bank", name=name)
 
@@ -167,6 +174,7 @@ def tile_layernormgrucell_w_kernel(
                 "dm": col(name + "_dm"),
                 "negmean": col(name + "_negmean"),
                 "kk": col(name + "_kk"),
+                "rstd": col(name + "_rstd"),
             }
 
         def evac(grp, k, acc, ys, bcol, n):
@@ -205,23 +213,15 @@ def tile_layernormgrucell_w_kernel(
                 scalar2=rs[:, 0:1], op0=ALU.mult, op1=ALU.add,
             )
 
-        def stats_early_sq(grp, nearly, times=None):
+        def stats_early_sq(grp):
             rq = col(grp["name"] + "_rq")
-            nc.vector.reduce_sum(out=rq[:], in_=grp["sq"][:, 0:nearly], axis=AX.X)
-            if times is None:
-                nc.vector.tensor_scalar(
-                    out=grp["aa"][:], in0=rq[:], scalar1=-grp["inv_n"], scalar2=EPS,
-                    op0=ALU.mult, op1=ALU.subtract,
-                )
-            else:
-                a0 = col(grp["name"] + "_a0")
-                nc.vector.tensor_scalar(
-                    out=a0[:], in0=rq[:], scalar1=-grp["inv_n"], scalar2=EPS,
-                    op0=ALU.mult, op1=ALU.subtract,
-                )
-                nc.vector.tensor_tensor(
-                    out=grp["aa"][:], in0=a0[:], in1=times[:], op=ALU.mult
-                )
+            nc.vector.reduce_sum(
+                out=rq[:], in_=grp["sq"][:, 0 : grp["nsq"] - 1], axis=AX.X
+            )
+            nc.vector.tensor_scalar(
+                out=grp["aa"][:], in0=rq[:], scalar1=-grp["inv_n"], scalar2=EPS,
+                op0=ALU.mult, op1=ALU.subtract,
+            )
 
         def stats_dm(grp, dst, factor):
             last = grp["nsum"] - 1
@@ -243,12 +243,12 @@ def tile_layernormgrucell_w_kernel(
                 op0=ALU.mult, op1=ALU.add,
             )
 
-        def stats_final(grp, dst, factor):
+        def stats_rsqrt(grp, negfactor):
             last = grp["nsq"] - 1
-            nc.vector.tensor_scalar(
-                out=dst, in0=grp["sq"][:, last : last + 1],
-                scalar1=factor, scalar2=grp["kk"][:, 0:1],
-                op0=ALU.mult, op1=ALU.subtract,
+            nc.scalar.activation(
+                out=grp["rstd"][:], in_=grp["sq"][:, last : last + 1],
+                func=ACT.Abs_reciprocal_sqrt,
+                bias=grp["kk"][:, 0:1], scale=negfactor,
             )
 
         def run_block(name, words, planes, op, wcol0, grp, c0, q0, y, boff, last):
@@ -285,8 +285,9 @@ def tile_layernormgrucell_w_kernel(
                 ev(3)
                 square(grp, q0 + 2, y[:, CH * (c0 + 3) : CH * (c0 + 4)], CH)
                 stats_dm(grp, grp["dm"][:], grp["inv_n"])
-                stats_early_sq(grp, grp["nsq"] - 1)
+                stats_early_sq(grp)
                 stats_kk(grp, grp["dm"][:, 0:1])
+                stats_rsqrt(grp, -grp["inv_n"])
                 stats_negmean(grp)
 
         yxg = const.tile([P, 2 * H], F32, name="yxg")
@@ -299,57 +300,42 @@ def tile_layernormgrucell_w_kernel(
         g_xg = make_group("xg", 8, 5, 2 * H)
         g_hg = make_group("hg", 8, 5, 2 * H)
         g_hn = make_group("hn", 4, 2, H)
-        g_xn = make_group("xn", 5, 5, H)
+        g_xn = make_group("xn", 5, 4, H)
 
-        def gate_stats(grp):
-            nm = grp["name"]
-            veps = col(nm + "_veps")
-            rstd = col(nm + "_rstd")
-            stats_final(grp, veps[:], grp["inv_n"])
-            nc.gpsimd.tensor_tensor(
-                out=rstd[:], in0=veps[:], in1=mhalf[:, 0:1], op=ALU.pow
-            )
-            return rstd
-
-        def times_rstd(name, grp, rstd):
+        def times_rstd(name, grp):
             nb = col(name)
             nc.vector.tensor_tensor(
-                out=nb[:], in0=grp["negmean"][:], in1=rstd[:], op=ALU.mult
+                out=nb[:], in0=grp["negmean"][:], in1=grp["rstd"][:], op=ALU.mult
             )
             return nb
 
         run_block("xg0", wi_words, planes_i, op_x, 0, g_xg, 0, 0, yxg, 0, False)
         run_block("xg1", wi_words, planes_i, op_x, BLK, g_xg, 4, 2, yxg, 0, True)
-        rstd_xg = gate_stats(g_xg)
-        nb_xg = times_rstd("xg_nb", g_xg, rstd_xg)
+        nb_xg = times_rstd("xg_nb", g_xg)
         for hf in range(2):
             sl = yxg[:, H * hf : H * (hf + 1)]
             nc.scalar.activation(
                 out=sl, in_=sl, func=ACT.Identity,
-                bias=nb_xg[:, 0:1], scale=rstd_xg[:, 0:1],
+                bias=nb_xg[:, 0:1], scale=g_xg["rstd"][:, 0:1],
             )
 
         run_block("hg0", wh_words, planes_h, op_h, 0, g_hg, 0, 0, yhg, NOUT, False)
         run_block("hg1", wh_words, planes_h, op_h, BLK, g_hg, 4, 2, yhg, NOUT, True)
-        rstd_hg = gate_stats(g_hg)
 
         acc_hn = [bank("hn_%d" % j) for j in range(4)]
-        for g in range(KG):
-            wt = load_g("w_hn_%d" % g, wh_words, g, 2 * H, BLK)
-            for j in range(4):
-                mx_pass(acc_hn[j], op_h, g, wt[:, 4 * CH * j : 4 * CH * (j + 1)],
-                        planes_h, 2 * H + CH * j, CH)
+        two_banks("w_hn_a", acc_hn[0:2], wh_words, planes_h, op_h, 2 * H)
+        two_banks("w_hn_b", acc_hn[2:4], wh_words, planes_h, op_h, 2 * H + 2 * CH)
 
         nb_hg = None
-        for pc in (2, 3, 0, 1):
+        for pc in range(4):
             sl = yhg[:, 1024 * pc : 1024 * (pc + 1)]
             nc.vector.scalar_tensor_tensor(
-                out=sl, in0=sl, scalar=rstd_hg[:, 0:1],
+                out=sl, in0=sl, scalar=g_hg["rstd"][:, 0:1],
                 in1=yxg[:, 1024 * pc : 1024 * (pc + 1)],
                 op0=ALU.mult, op1=ALU.add,
             )
             if nb_hg is None:
-                nb_hg = times_rstd("hg_nb", g_hg, rstd_hg)
+                nb_hg = times_rstd("hg_nb", g_hg)
             nc.scalar.activation(
                 out=sl, in_=sl, func=ACT.Sigmoid, bias=nb_hg[:, 0:1], scale=1.0
             )
@@ -362,10 +348,19 @@ def tile_layernormgrucell_w_kernel(
                 nc.gpsimd.tensor_tensor(
                     out=zh[:, cs], in0=sl, in1=hx_sb[:, cs], op=ALU.mult
                 )
+        warm3 = col("warm3")
+        nc.scalar.activation(out=warm3[:], in_=warm[:], func=ACT.Abs_reciprocal_sqrt)
 
         def ev_hn(c):
             evac(g_hn, c, acc_hn[c], yhn[:, CH * c : CH * (c + 1)],
                  NOUT + 2 * H + CH * c, CH)
+
+        def q_piece(pc):
+            cs = slice(1024 * pc, 1024 * (pc + 1))
+            nc.vector.scalar_tensor_tensor(
+                out=qn[:, cs], in0=yhn[:, cs], scalar=g_hn["negmean"][:, 0:1],
+                in1=yhg[:, cs], op0=ALU.add, op1=ALU.mult,
+            )
 
         ev_hn(0)
         ev_hn(1)
@@ -376,69 +371,60 @@ def tile_layernormgrucell_w_kernel(
         square(g_hn, 1, yhn[:, 2 * CH : 4 * CH], 2 * CH)
         stats_dm(g_hn, g_hn["dm"][:], g_hn["inv_n"])
         stats_negmean(g_hn)
-        for pc in range(2):
-            cs = slice(1024 * pc, 1024 * (pc + 1))
-            nc.vector.scalar_tensor_tensor(
-                out=qn[:, cs], in0=yhn[:, cs], scalar=g_hn["negmean"][:, 0:1],
-                in1=yhg[:, cs], op0=ALU.add, op1=ALU.mult,
-            )
+        q_piece(0)
+        stats_early_sq(g_hn)
+        stats_kk(g_hn, g_hn["dm"][:, 0:1])
+        stats_rsqrt(g_hn, -g_hn["inv_n"])
+        q_piece(1)
+        rstd_hn = g_hn["rstd"]
+        inv_hn = col("hn_inv")
+        negfac = col("xn_negfac")
+        dsc = col("xn_dsc")
+        nc.vector.tensor_tensor(out=inv_hn[:], in0=rstd_hn[:], in1=rstd_hn[:], op=ALU.mult)
+        nc.vector.tensor_scalar_mul(out=dsc[:], in0=rstd_hn[:], scalar1=g_xn["inv_n"])
+        nc.vector.tensor_scalar_mul(out=negfac[:], in0=inv_hn[:], scalar1=-g_xn["inv_n"])
 
         chunks = ((0, 512), (512, 512), (1024, 512), (1536, 256), (1792, 256))
         acc_xn = [bank("xn_%d" % k) for k in range(5)]
-        veps_hn = col("hn_veps")
-        rstd_hn = col("hn_rstd")
-        inv_hn = col("hn_inv")
-        fac_xn = col("xn_fac")
-        negfac_xn = col("xn_negfac")
-        dsc_xn = col("xn_dsc")
+        sums = g_xn["sums"]
+        sq = g_xn["sq"]
+        u01 = col("xn_u01")
+        e01 = col("xn_e01")
         dms = col("xn_dms")
-        ratio = col("xn_ratio")
-        rho = col("xn_rho")
-        for hf in range(2):
-            wt = load_gs("w_xn_a%d" % hf, wi_words, 2 * hf, 2, 2 * H, 2 * CH)
-            for k in range(2):
-                for gg in range(2):
-                    mx_pass(acc_xn[k], op_x, 2 * hf + gg,
-                            wt[:, gg, 4 * CH * k : 4 * CH * (k + 1)],
-                            planes_i, 2 * H + CH * k, CH)
+        two_banks("w_xn_a", acc_xn[0:2], wi_words, planes_i, op_x, 2 * H)
         for k in range(5):
             cc, n = chunks[k]
             if k >= 2:
                 wt = load_gs("w_xn_%d" % k, wi_words, 0, KG, 2 * H + cc, n)
                 for g in range(KG):
                     mx_pass(acc_xn[k], op_x, g, wt[:, g, :], planes_i, 2 * H + cc, n)
-            if k == 4:
-                stats_early_sum(g_xn)
             evac(g_xn, k, acc_xn[k], yxn[:, cc : cc + n], 2 * H + cc, n)
-            square(g_xn, k, yxn[:, cc : cc + n], n)
+            if k < 3:
+                square(g_xn, k, yxn[:, cc : cc + n], n)
             if k == 1:
-                stats_early_sq(g_hn, 1)
-                stats_kk(g_hn, g_hn["dm"][:, 0:1])
-                stats_final(g_hn, veps_hn[:], g_hn["inv_n"])
-                nc.gpsimd.tensor_tensor(
-                    out=rstd_hn[:], in0=veps_hn[:], in1=mhalf[:, 0:1], op=ALU.pow
+                nc.vector.tensor_scalar(
+                    out=u01[:], in0=sums[:, 0:1], scalar1=1.0 - H / CH,
+                    scalar2=sums[:, 1:2], op0=ALU.mult, op1=ALU.add,
                 )
             if k == 2:
-                nc.vector.reciprocal(out=inv_hn[:], in_=veps_hn[:])
-                nc.vector.tensor_scalar_mul(
-                    out=fac_xn[:], in0=inv_hn[:], scalar1=g_xn["inv_n"]
-                )
-                nc.vector.tensor_scalar_mul(
-                    out=negfac_xn[:], in0=inv_hn[:], scalar1=-g_xn["inv_n"]
+                nc.vector.tensor_scalar(
+                    out=e01[:], in0=sq[:, 0:1], scalar1=H * EPS,
+                    scalar2=sq[:, 1:2], op0=ALU.add, op1=ALU.add,
                 )
             if k == 3:
-                stats_early_sq(g_xn, 3, times=inv_hn)
-                nc.vector.tensor_scalar_mul(
-                    out=dsc_xn[:], in0=rstd_hn[:], scalar1=g_xn["inv_n"]
+                nc.vector.tensor_scalar(
+                    out=g_xn["totp"][:], in0=sums[:, 2:3], scalar1=u01[:, 0:1],
+                    scalar2=sums[:, 3:4], op0=ALU.add, op1=ALU.add,
                 )
-        stats_dm(g_xn, dms[:], dsc_xn[:, 0:1])
-        nc.vector.scalar_tensor_tensor(
-            out=g_xn["aa"][:], in0=g_xn["sq"][:, 3:4], scalar=negfac_xn[:, 0:1],
-            in1=g_xn["aa"][:], op0=ALU.mult, op1=ALU.add,
+        square(g_xn, 3, yxn[:, 1536:2048], 512)
+        stats_dm(g_xn, dms[:], dsc[:, 0:1])
+        nc.vector.tensor_scalar(
+            out=g_xn["aa"][:], in0=sq[:, 2:3], scalar1=e01[:, 0:1],
+            scalar2=negfac[:, 0:1], op0=ALU.add, op1=ALU.mult,
         )
         stats_kk(g_xn, dms[:, 0:1])
-        stats_final(g_xn, ratio[:], fac_xn[:, 0:1])
-        nc.gpsimd.tensor_tensor(out=rho[:], in0=ratio[:], in1=mhalf[:, 0:1], op=ALU.pow)
+        stats_rsqrt(g_xn, negfac[:, 0:1])
+        rho = g_xn["rstd"]
         stats_dm(g_xn, g_xn["dm"][:], g_xn["inv_n"])
         stats_negmean(g_xn)
         nb = col("xn_nb")
@@ -478,15 +464,15 @@ def tile_layernormgrucell_w_kernel(
         p2(1)
         p1(2)
         p2(2)
-        p3(0)
         p1(3)
         p2(3)
-        p4(0)
-        p3(1)
         p1(4)
         p2(4)
-        p4(1)
+        p3(0)
+        p3(1)
+        p4(0)
         p3(2)
+        p4(1)
         p3(3)
         p4(2)
         p3(4)

@@ -50,8 +50,6 @@ def tile_layernormgrucell_w_kernel(
         nc.vector.memset(planes_h[:].bitcast(I32), 0)
         ident_f = const.tile([P, P], F32, name="ident_f")
         make_identity(nc, ident_f[:])
-        ident_b = const.tile([P, P], BF16, name="ident_b")
-        make_identity(nc, ident_b[:])
 
         x_sb = const.tile([P, DI], BF16, name="x_sb", align_bytes=64)
         hx_sb = const.tile([P, H], BF16, name="hx_sb", align_bytes=64)
@@ -62,11 +60,13 @@ def tile_layernormgrucell_w_kernel(
         warm2 = col("warm2")
         nc.scalar.activation(out=warm2[:], in_=warm[:], func=ACT.Abs_reciprocal_sqrt)
         for planes, scales in ((planes_i, wi_scales), (planes_h, wh_scales)):
-            for q in range(4):
-                nc.sync.dma_start(
-                    out=planes[32 * q : 32 * q + 16, :].bitcast(I32),
-                    in_=scales[:, 4 * q : 4 * q + 4, :].bitcast(I32),
+            for q in (0, 2, 1, 3):
+                nc.gpsimd.dma_start(
+                    out=planes[32 * q : 32 * q + 16, :].bitcast(F32),
+                    in_=scales[:, 4 * q : 4 * q + 4, :].bitcast(F32),
                 )
+        ident_b = const.tile([P, P], BF16, name="ident_b")
+        make_identity(nc, ident_b[:])
 
         ops = []
         for nm, src in (("x", x_sb), ("h", hx_sb)):

@@ -50,6 +50,8 @@ def tile_layernormgrucell_w_kernel(
         nc.vector.memset(planes_h[:].bitcast(I32), 0)
         ident_f = const.tile([P, P], F32, name="ident_f")
         make_identity(nc, ident_f[:])
+        ident_b = const.tile([P, P], BF16, name="ident_b")
+        make_identity(nc, ident_b[:])
 
         x_sb = const.tile([P, DI], BF16, name="x_sb", align_bytes=64)
         hx_sb = const.tile([P, H], BF16, name="hx_sb", align_bytes=64)
@@ -60,13 +62,11 @@ def tile_layernormgrucell_w_kernel(
         warm2 = col("warm2")
         nc.scalar.activation(out=warm2[:], in_=warm[:], func=ACT.Abs_reciprocal_sqrt)
         for planes, scales in ((planes_i, wi_scales), (planes_h, wh_scales)):
-            for q in (0, 2, 1, 3):
-                nc.gpsimd.dma_start(
-                    out=planes[32 * q : 32 * q + 16, :].bitcast(F32),
-                    in_=scales[:, 4 * q : 4 * q + 4, :].bitcast(F32),
+            for q in range(4):
+                nc.sync.dma_start(
+                    out=planes[32 * q : 32 * q + 16, :].bitcast(I32),
+                    in_=scales[:, 4 * q : 4 * q + 4, :].bitcast(I32),
                 )
-        ident_b = const.tile([P, P], BF16, name="ident_b")
-        make_identity(nc, ident_b[:])
 
         ops = []
         for nm, src in (("x", x_sb), ("h", hx_sb)):
@@ -327,6 +327,7 @@ def tile_layernormgrucell_w_kernel(
         two_banks("w_hn_b", acc_hn[2:4], wh_words, planes_h, op_h, 2 * H + 2 * CH)
 
         nb_hg = None
+        nnb_hg = col("hg_nnb")
         for pc in range(4):
             sl = yhg[:, 1024 * pc : 1024 * (pc + 1)]
             nc.vector.scalar_tensor_tensor(
@@ -336,17 +337,15 @@ def tile_layernormgrucell_w_kernel(
             )
             if nb_hg is None:
                 nb_hg = times_rstd("hg_nb", g_hg)
-            nc.scalar.activation(
-                out=sl, in_=sl, func=ACT.Sigmoid, bias=nb_hg[:, 0:1], scale=1.0
-            )
-            if pc >= 2:
-                cs = slice(1024 * (pc - 2), 1024 * (pc - 1))
-                nc.gpsimd.tensor_scalar(
-                    out=omz[:, cs], in0=sl, scalar1=-1.0, scalar2=1.0,
-                    op0=ALU.mult, op1=ALU.add,
+                nc.vector.tensor_scalar_mul(out=nnb_hg[:], in0=nb_hg[:], scalar1=-1.0)
+            if pc < 2:
+                nc.scalar.activation(
+                    out=sl, in_=sl, func=ACT.Sigmoid, bias=nb_hg[:, 0:1], scale=1.0
                 )
-                nc.gpsimd.tensor_tensor(
-                    out=zh[:, cs], in0=sl, in1=hx_sb[:, cs], op=ALU.mult
+            else:
+                nc.scalar.activation(
+                    out=omz[:, 1024 * (pc - 2) : 1024 * (pc - 1)], in_=sl,
+                    func=ACT.Sigmoid, bias=nnb_hg[:, 0:1], scale=-1.0,
                 )
         warm3 = col("warm3")
         nc.scalar.activation(out=warm3[:], in_=warm[:], func=ACT.Abs_reciprocal_sqrt)
@@ -365,6 +364,12 @@ def tile_layernormgrucell_w_kernel(
         ev_hn(0)
         ev_hn(1)
         square(g_hn, 0, yhn[:, 0 : 2 * CH], 2 * CH)
+        for pc in range(2):
+            cs = slice(1024 * pc, 1024 * (pc + 1))
+            nc.vector.scalar_tensor_tensor(
+                out=zh[:, cs], in0=omz[:, cs], scalar=1.0, in1=hx_sb[:, cs],
+                op0=ALU.subtract, op1=ALU.mult,
+            )
         ev_hn(2)
         stats_early_sum(g_hn)
         ev_hn(3)
@@ -451,7 +456,7 @@ def tile_layernormgrucell_w_kernel(
         def p4(j):
             cc, n = chunks[j]
             sl = yxn[:, cc : cc + n]
-            nc.vector.tensor_tensor(out=sl, in0=sl, in1=zh[:, cc : cc + n], op=ALU.add)
+            nc.vector.tensor_tensor(out=sl, in0=sl, in1=zh[:, cc : cc + n], op=ALU.subtract)
             nc.sync.dma_start(out=out[:, cc : cc + n], in_=sl)
 
         p1(0)

@@ -385,9 +385,6 @@ def tile_layernormgrucell_w_kernel(
         inv_hn = col("hn_inv")
         negfac = col("xn_negfac")
         dsc = col("xn_dsc")
-        nc.vector.tensor_tensor(out=inv_hn[:], in0=rstd_hn[:], in1=rstd_hn[:], op=ALU.mult)
-        nc.vector.tensor_scalar_mul(out=dsc[:], in0=rstd_hn[:], scalar1=g_xn["inv_n"])
-        nc.vector.tensor_scalar_mul(out=negfac[:], in0=inv_hn[:], scalar1=-g_xn["inv_n"])
 
         chunks = ((0, 512), (512, 512), (1024, 512), (1536, 256), (1792, 256))
         acc_xn = [bank("xn_%d" % k) for k in range(5)]
@@ -397,12 +394,21 @@ def tile_layernormgrucell_w_kernel(
         e01 = col("xn_e01")
         dms = col("xn_dms")
         two_banks("w_xn_a", acc_xn[0:2], wi_words, planes_i, op_x, 2 * H)
+        wt = load_gs("w_xn_b", wi_words, 0, KG, 2 * H + 1024, CH)
+        for g in range(KG):
+            mx_pass(acc_xn[2], op_x, g, wt[:, g, :], planes_i, 2 * H + 1024, CH)
+        wt = load_gs("w_xn_c", wi_words, 0, KG - 1, 2 * H + 1536, CH)
+        for k in (3, 4):
+            cc, n = chunks[k]
+            for g in range(KG - 1):
+                mx_pass(acc_xn[k], op_x, g, wt[:, g, 4 * (cc - 1536) : 4 * (cc - 1536 + n)],
+                        planes_i, 2 * H + cc, n)
+        for k in (3, 4):
+            cc, n = chunks[k]
+            wt = load_g("w_xn_l%d" % k, wi_words, KG - 1, 2 * H + cc, n)
+            mx_pass(acc_xn[k], op_x, KG - 1, wt[:, :], planes_i, 2 * H + cc, n)
         for k in range(5):
             cc, n = chunks[k]
-            if k >= 2:
-                wt = load_gs("w_xn_%d" % k, wi_words, 0, KG, 2 * H + cc, n)
-                for g in range(KG):
-                    mx_pass(acc_xn[k], op_x, g, wt[:, g, :], planes_i, 2 * H + cc, n)
             evac(g_xn, k, acc_xn[k], yxn[:, cc : cc + n], 2 * H + cc, n)
             if k < 3:
                 square(g_xn, k, yxn[:, cc : cc + n], n)
@@ -411,10 +417,14 @@ def tile_layernormgrucell_w_kernel(
                     out=u01[:], in0=sums[:, 0:1], scalar1=1.0 - H / CH,
                     scalar2=sums[:, 1:2], op0=ALU.mult, op1=ALU.add,
                 )
-            if k == 2:
-                nc.vector.tensor_scalar(
-                    out=e01[:], in0=sq[:, 0:1], scalar1=H * EPS,
-                    scalar2=sq[:, 1:2], op0=ALU.add, op1=ALU.add,
+                nc.vector.tensor_tensor(
+                    out=inv_hn[:], in0=rstd_hn[:], in1=rstd_hn[:], op=ALU.mult
+                )
+                nc.vector.tensor_scalar_mul(
+                    out=dsc[:], in0=rstd_hn[:], scalar1=g_xn["inv_n"]
+                )
+                nc.vector.tensor_scalar_mul(
+                    out=negfac[:], in0=inv_hn[:], scalar1=-g_xn["inv_n"]
                 )
             if k == 3:
                 nc.vector.tensor_scalar(
@@ -422,6 +432,10 @@ def tile_layernormgrucell_w_kernel(
                     scalar2=sums[:, 3:4], op0=ALU.add, op1=ALU.add,
                 )
         square(g_xn, 3, yxn[:, 1536:2048], 512)
+        nc.vector.tensor_scalar(
+            out=e01[:], in0=sq[:, 0:1], scalar1=H * EPS,
+            scalar2=sq[:, 1:2], op0=ALU.add, op1=ALU.add,
+        )
         stats_dm(g_xn, dms[:], dsc[:, 0:1])
         nc.vector.tensor_scalar(
             out=g_xn["aa"][:], in0=sq[:, 2:3], scalar1=e01[:, 0:1],

@@ -30,7 +30,6 @@ def tile_layernormgrucell_w_kernel(
 ):
     nc = tc.nc
     with ExitStack() as ctx:
-        ctx.enter_context(tc.manual_schedule())
         const = ctx.enter_context(tc.tile_pool(name="const", bufs=1))
         small = ctx.enter_context(tc.tile_pool(name="small", bufs=1))
         wpool = ctx.enter_context(tc.tile_pool(name="wpool", bufs=11))

from contextlib import ExitStack

import concourse.mybir as mybir
from concourse.masks import make_identity

F32 = mybir.dt.float32
BF16 = mybir.dt.bfloat16
I32 = mybir.dt.int32
U8 = mybir.dt.uint8
U32 = mybir.dt.uint32
FP8X4 = mybir.dt.float8_e4m3fn_x4
ALU = mybir.AluOpType
ACT = mybir.ActivationFunctionType
AX = mybir.AxisListType

P = 128
DI = 2048
H = 2048
NOUT = 3 * H
KG = DI // 512
CH = 512
BLK = 2048
EPS = 1e-5

FLOPS = 2 * 2 * P * DI * NOUT


def tile_layernormgrucell_w_kernel(
    tc, x, hx, wi_words, wi_scales, b_i, wh_words, wh_scales, b_h, out
):
    nc = tc.nc
    with ExitStack() as ctx:
        const = ctx.enter_context(tc.tile_pool(name="const", bufs=1))
        small = ctx.enter_context(tc.tile_pool(name="small", bufs=1))
        wpool = ctx.enter_context(tc.tile_pool(name="wpool", bufs=11))
        junkp = ctx.enter_context(tc.tile_pool(name="junkp", bufs=2))
        psum = ctx.enter_context(tc.psum_pool(name="psum", bufs=8))

        def col(name, width=1):
            return small.tile([P, width], F32, name=name)

        brows = const.tile([P, CH], BF16, name="brows")
        nc.vector.memset(brows[:], 0.0)
        warm = col("warm")
        nc.vector.memset(warm[:], 1.0)
        planes_i = const.tile([P, NOUT], U8, name="planes_i", align_bytes=64)
        planes_h = const.tile([P, NOUT], U8, name="planes_h", align_bytes=64)
        nc.vector.memset(planes_i[:].bitcast(I32), 0)
        nc.vector.memset(planes_h[:].bitcast(I32), 0)
        ident_f = const.tile([P, P], F32, name="ident_f")
        make_identity(nc, ident_f[:])
        ident_b = const.tile([P, P], BF16, name="ident_b")
        make_identity(nc, ident_b[:])

        x_sb = const.tile([P, DI], BF16, name="x_sb", align_bytes=64)
        hx_sb = const.tile([P, H], BF16, name="hx_sb", align_bytes=64)
        nc.sync.dma_start(out=x_sb[:], in_=x[:, :])
        nc.sync.dma_start(out=hx_sb[:], in_=hx[:, :])
        nc.scalar.dma_start(out=brows[0:12, :], in_=b_i.rearrange("(r c) -> r c", c=CH))
        nc.scalar.dma_start(out=brows[12:24, :], in_=b_h.rearrange("(r c) -> r c", c=CH))
        warm2 = col("warm2")
        nc.scalar.activation(out=warm2[:], in_=warm[:], func=ACT.Abs_reciprocal_sqrt)
        for planes, scales in ((planes_i, wi_scales), (planes_h, wh_scales)):
            for q in range(4):
                nc.sync.dma_start(
                    out=planes[32 * q : 32 * q + 16, :].bitcast(I32),
                    in_=scales[:, 4 * q : 4 * q + 4, :].bitcast(I32),
                )

        ops = []
        for nm, src in (("x", x_sb), ("h", hx_sb)):
            words = src[:].bitcast(F32)
            grouped = const.tile([P, DI], BF16, name="grouped_" + nm, align_bytes=64)
            gw = grouped[:].bitcast(F32)
            for hf in range(2):
                tp = psum.tile([P, 4, P], F32, tag="bank", name="tp_%s%d" % (nm, hf))
                for gg in range(2):
                    g = 2 * hf + gg
                    for u in range(2):
                        nc.tensor.transpose(
                            tp[:, 2 * gg + u, :],
                            words[:, 256 * g + u : 256 * (g + 1) : 2],
                            ident_f[:],
                        )
                dst = gw[:, 512 * hf : 512 * (hf + 1)].rearrange(
                    "p (g b u) -> p g b u", g=2, u=2
                )
                srcv = tp[:].rearrange("p (g u) b -> p g b u", g=2)
                if hf == 0:
                    nc.vector.tensor_copy(out=dst, in_=srcv)
                else:
                    nc.scalar.copy(out=dst, in_=srcv)
            codes = const.tile([P, KG * P], U32, name="codes_" + nm, align_bytes=64)
            cscale = const.tile([P, KG * P], U8, name="cscale_" + nm, align_bytes=64)
            ops.append((grouped, codes, cscale))
        for grouped, codes, cscale in ops:
            nc.vector.quantize_mx(
                out=codes[:].bitcast(FP8X4), scales=cscale[:], in_=grouped[:]
            )
        op_x = (ops[0][1], ops[0][2])
        op_h = (ops[1][1], ops[1][2])

        bias_sb = const.tile([P, 2 * NOUT], BF16, name="bias_sb")
        for i in range(12):
            bp = psum.tile([P, 2 * CH], BF16, tag="bank", name="bp%d" % i)
            for hf in range(2):
                j = 2 * i + hf
                nc.tensor.matmul(
                    out=bp[:, CH * hf : CH * (hf + 1)],
                    lhsT=ident_b[:, j : j + 1].to_broadcast([P, P]),
                    rhs=brows[:],
                    start=True,
                    stop=True,
                )
            nc.scalar.copy(out=bias_sb[:, 2 * CH * i : 2 * CH * (i + 1)], in_=bp[:])

        def load_g(name, words, g, c0, ncols):
            wt = wpool.tile([P, 4 * ncols], U8, tag="w", name=name, align_bytes=64)
            nc.sync.dma_start(
                out=wt[:].bitcast(I32),
                in_=words[g, :, c0 : c0 + ncols, :]
                .rearrange("p n t -> p (n t)")
                .bitcast(I32),
            )
            return wt

        def load_gs(name, words, g0, ng, c0, ncols):
            wt = wpool.tile([P, ng, 4 * ncols], U8, tag="w", name=name, align_bytes=64)
            nc.sync.dma_start(
                out=wt[:].bitcast(I32),
                in_=words[g0 : g0 + ng, :, c0 : c0 + ncols, :]
                .rearrange("g p n t -> p g (n t)")
                .bitcast(I32),
            )
            return wt

        def mx_pass(acc, op, g, rhs, planes, pcol, n):
            codes, cscale = op
            nc.tensor.matmul_mx(
                out=acc[:, 0:n],
                lhsT=codes[:, P * g : P * (g + 1)].bitcast(FP8X4),
                lhsT_scale=cscale[:, P * g : P * (g + 1)],
                rhs=rhs.bitcast(FP8X4),
                rhs_scale=planes[4 * g : P, pcol : pcol + n],
                start=(g == 0),
                stop=(g == KG - 1),
            )

        def two_banks(name, accs, words, planes, op, wcol0):
            for hf in range(2):
                wt = load_gs("%s%d" % (name, hf), words, 2 * hf, 2, wcol0, 2 * CH)
                for k in range(2):
                    for gg in range(2):
                        mx_pass(accs[k], op, 2 * hf + gg,
                                wt[:, gg, 4 * CH * k : 4 * CH * (k + 1)],
                                planes, wcol0 + CH * k, CH)

        def bank(name):
            return psum.tile([P, CH], F32, tag="bank", name=name)

        def make_group(name, nsum, nsq, ncols):
            return {
                "name": name,
                "ncols": ncols,
                "inv_n": 1.0 / ncols,
                "nsum": nsum,
                "nsq": nsq,
                "sums": col(name + "_sums", nsum),
                "sq": col(name + "_sq", nsq),
                "negc": col(name + "_negc"),
                "totp": col(name + "_totp"),
                "aa": col(name + "_aa"),
                "dm": col(name + "_dm"),
                "negmean": col(name + "_negmean"),
                "kk": col(name + "_kk"),
                "rstd": col(name + "_rstd"),
            }

        def evac(grp, k, acc, ys, bcol, n):
            nc.vector.scalar_tensor_tensor(
                out=ys,
                in0=acc[:, 0:n],
                scalar=1.0,
                in1=bias_sb[:, bcol : bcol + n],
                op0=ALU.mult,
                op1=ALU.add,
                accum_out=grp["sums"][:, k : k + 1],
            )
            if k == 0:
                nc.vector.tensor_scalar_mul(
                    out=grp["negc"][:], in0=grp["sums"][:, 0:1], scalar1=-1.0 / n
                )

        def square(grp, k, ys, n):
            junk = junkp.tile([P, 2 * CH], F32, tag="junk", name="junk_%s%d" % (grp["name"], k))
            nc.scalar.activation(
                out=junk[:, 0:n],
                in_=ys,
                func=ACT.Square,
                bias=grp["negc"][:, 0:1],
                scale=1.0,
                accum_out=grp["sq"][:, k : k + 1],
            )

        def stats_early_sum(grp):
            rs = col(grp["name"] + "_rs")
            nc.vector.reduce_sum(
                out=rs[:], in_=grp["sums"][:, 0 : grp["nsum"] - 1], axis=AX.X
            )
            nc.vector.tensor_scalar(
                out=grp["totp"][:], in0=grp["negc"][:], scalar1=float(grp["ncols"]),
                scalar2=rs[:, 0:1], op0=ALU.mult, op1=ALU.add,
            )

        def stats_early_sq(grp):
            rq = col(grp["name"] + "_rq")
            nc.vector.reduce_sum(
                out=rq[:], in_=grp["sq"][:, 0 : grp["nsq"] - 1], axis=AX.X
            )
            nc.vector.tensor_scalar(
                out=grp["aa"][:], in0=rq[:], scalar1=-grp["inv_n"], scalar2=EPS,
                op0=ALU.mult, op1=ALU.subtract,
            )

        def stats_dm(grp, dst, factor):
            last = grp["nsum"] - 1
            nc.vector.tensor_scalar(
                out=dst, in0=grp["sums"][:, last : last + 1],
                scalar1=grp["totp"][:, 0:1], scalar2=factor,
                op0=ALU.add, op1=ALU.mult,
            )

        def stats_negmean(grp):
            nc.vector.tensor_tensor(
                out=grp["negmean"][:], in0=grp["negc"][:], in1=grp["dm"][:],
                op=ALU.subtract,
            )

        def stats_kk(grp, d):
            nc.vector.scalar_tensor_tensor(
                out=grp["kk"][:], in0=d, scalar=d, in1=grp["aa"][:],
                op0=ALU.mult, op1=ALU.add,
            )

        def stats_rsqrt(grp, negfactor):
            last = grp["nsq"] - 1
            nc.scalar.activation(
                out=grp["rstd"][:], in_=grp["sq"][:, last : last + 1],
                func=ACT.Abs_reciprocal_sqrt,
                bias=grp["kk"][:, 0:1], scale=negfactor,
            )

        def run_block(name, words, planes, op, wcol0, grp, c0, q0, y, boff, last):
            accs = [bank("%s_%d" % (name, j)) for j in range(BLK // CH)]
            for g in range(KG - 1):
                wt = load_g("w_%s_%d" % (name, g), words, g, wcol0, BLK)
                for j in range(BLK // CH):
                    mx_pass(accs[j], op, g, wt[:, 4 * CH * j : 4 * CH * (j + 1)],
                            planes, wcol0 + CH * j, CH)
            g = KG - 1
            split = 2 if last else 1
            per = BLK // split
            for s in range(split):
                wt = load_g("w_%s_%d_%d" % (name, g, s), words, g, wcol0 + per * s, per)
                for jj in range(per // CH):
                    j = s * (per // CH) + jj
                    mx_pass(accs[j], op, g, wt[:, 4 * CH * jj : 4 * CH * (jj + 1)],
                            planes, wcol0 + CH * j, CH)

            def ev(j):
                c = c0 + j
                evac(grp, c, accs[j], y[:, CH * c : CH * (c + 1)], boff + CH * c, CH)

            ev(0)
            ev(1)
            square(grp, q0, y[:, CH * c0 : CH * (c0 + 2)], 2 * CH)
            ev(2)
            if not last:
                ev(3)
                square(grp, q0 + 1, y[:, CH * (c0 + 2) : CH * (c0 + 4)], 2 * CH)
            else:
                square(grp, q0 + 1, y[:, CH * (c0 + 2) : CH * (c0 + 3)], CH)
                stats_early_sum(grp)
                ev(3)
                square(grp, q0 + 2, y[:, CH * (c0 + 3) : CH * (c0 + 4)], CH)
                stats_dm(grp, grp["dm"][:], grp["inv_n"])
                stats_early_sq(grp)
                stats_kk(grp, grp["dm"][:, 0:1])
                stats_rsqrt(grp, -grp["inv_n"])
                stats_negmean(grp)

        yxg = const.tile([P, 2 * H], F32, name="yxg")
        yhg = const.tile([P, 2 * H], F32, name="yhg")
        yhn = const.tile([P, H], F32, name="yhn")
        yxn = const.tile([P, H], F32, name="yxn")
        qn = const.tile([P, H], F32, name="qn")
        omz = const.tile([P, H], F32, name="omz")
        zh = const.tile([P, H], F32, name="zh")
        g_xg = make_group("xg", 8, 5, 2 * H)
        g_hg = make_group("hg", 8, 5, 2 * H)
        g_hn = make_group("hn", 4, 2, H)
        g_xn = make_group("xn", 5, 4, H)

        def times_rstd(name, grp):
            nb = col(name)
            nc.vector.tensor_tensor(
                out=nb[:], in0=grp["negmean"][:], in1=grp["rstd"][:], op=ALU.mult
            )
            return nb

        run_block("xg0", wi_words, planes_i, op_x, 0, g_xg, 0, 0, yxg, 0, False)
        run_block("xg1", wi_words, planes_i, op_x, BLK, g_xg, 4, 2, yxg, 0, True)
        nb_xg = times_rstd("xg_nb", g_xg)
        for hf in range(2):
            sl = yxg[:, H * hf : H * (hf + 1)]
            nc.scalar.activation(
                out=sl, in_=sl, func=ACT.Identity,
                bias=nb_xg[:, 0:1], scale=g_xg["rstd"][:, 0:1],
            )

        run_block("hg0", wh_words, planes_h, op_h, 0, g_hg, 0, 0, yhg, NOUT, False)
        run_block("hg1", wh_words, planes_h, op_h, BLK, g_hg, 4, 2, yhg, NOUT, True)

        acc_hn = [bank("hn_%d" % j) for j in range(4)]
        two_banks("w_hn_a", acc_hn[0:2], wh_words, planes_h, op_h, 2 * H)
        two_banks("w_hn_b", acc_hn[2:4], wh_words, planes_h, op_h, 2 * H + 2 * CH)

        nb_hg = None
        nnb_hg = col("hg_nnb")
        for pc in range(4):
            sl = yhg[:, 1024 * pc : 1024 * (pc + 1)]
            nc.vector.scalar_tensor_tensor(
                out=sl, in0=sl, scalar=g_hg["rstd"][:, 0:1],
                in1=yxg[:, 1024 * pc : 1024 * (pc + 1)],
                op0=ALU.mult, op1=ALU.add,
            )
            if nb_hg is None:
                nb_hg = times_rstd("hg_nb", g_hg)
                nc.vector.tensor_scalar_mul(out=nnb_hg[:], in0=nb_hg[:], scalar1=-1.0)
            if pc < 2:
                nc.scalar.activation(
                    out=sl, in_=sl, func=ACT.Sigmoid, bias=nb_hg[:, 0:1], scale=1.0
                )
            else:
                nc.scalar.activation(
                    out=omz[:, 1024 * (pc - 2) : 1024 * (pc - 1)], in_=sl,
                    func=ACT.Sigmoid, bias=nnb_hg[:, 0:1], scale=-1.0,
                )
        warm3 = col("warm3")
        nc.scalar.activation(out=warm3[:], in_=warm[:], func=ACT.Abs_reciprocal_sqrt)

        def ev_hn(c):
            evac(g_hn, c, acc_hn[c], yhn[:, CH * c : CH * (c + 1)],
                 NOUT + 2 * H + CH * c, CH)

        def q_piece(pc):
            cs = slice(1024 * pc, 1024 * (pc + 1))
            nc.vector.scalar_tensor_tensor(
                out=qn[:, cs], in0=yhn[:, cs], scalar=g_hn["negmean"][:, 0:1],
                in1=yhg[:, cs], op0=ALU.add, op1=ALU.mult,
            )

        ev_hn(0)
        ev_hn(1)
        square(g_hn, 0, yhn[:, 0 : 2 * CH], 2 * CH)
        for pc in range(2):
            cs = slice(1024 * pc, 1024 * (pc + 1))
            nc.vector.scalar_tensor_tensor(
                out=zh[:, cs], in0=omz[:, cs], scalar=1.0, in1=hx_sb[:, cs],
                op0=ALU.subtract, op1=ALU.mult,
            )
        ev_hn(2)
        stats_early_sum(g_hn)
        ev_hn(3)
        square(g_hn, 1, yhn[:, 2 * CH : 4 * CH], 2 * CH)
        stats_dm(g_hn, g_hn["dm"][:], g_hn["inv_n"])
        stats_negmean(g_hn)
        q_piece(0)
        stats_early_sq(g_hn)
        stats_kk(g_hn, g_hn["dm"][:, 0:1])
        stats_rsqrt(g_hn, -g_hn["inv_n"])
        q_piece(1)
        rstd_hn = g_hn["rstd"]
        inv_hn = col("hn_inv")
        negfac = col("xn_negfac")
        dsc = col("xn_dsc")

        chunks = ((0, 512), (512, 512), (1024, 512), (1536, 256), (1792, 256))
        acc_xn = [bank("xn_%d" % k) for k in range(5)]
        sums = g_xn["sums"]
        sq = g_xn["sq"]
        u01 = col("xn_u01")
        e01 = col("xn_e01")
        dms = col("xn_dms")
        two_banks("w_xn_a", acc_xn[0:2], wi_words, planes_i, op_x, 2 * H)
        wt = load_gs("w_xn_b", wi_words, 0, KG, 2 * H + 1024, CH)
        for g in range(KG):
            mx_pass(acc_xn[2], op_x, g, wt[:, g, :], planes_i, 2 * H + 1024, CH)
        wt = load_gs("w_xn_c", wi_words, 0, KG - 1, 2 * H + 1536, CH)
        for k in (3, 4):
            cc, n = chunks[k]
            for g in range(KG - 1):
                mx_pass(acc_xn[k], op_x, g, wt[:, g, 4 * (cc - 1536) : 4 * (cc - 1536 + n)],
                        planes_i, 2 * H + cc, n)
        for k in (3, 4):
            cc, n = chunks[k]
            wt = load_g("w_xn_l%d" % k, wi_words, KG - 1, 2 * H + cc, n)
            mx_pass(acc_xn[k], op_x, KG - 1, wt[:, :], planes_i, 2 * H + cc, n)
        for k in range(5):
            cc, n = chunks[k]
            evac(g_xn, k, acc_xn[k], yxn[:, cc : cc + n], 2 * H + cc, n)
            if k < 3:
                square(g_xn, k, yxn[:, cc : cc + n], n)
            if k == 1:
                nc.vector.tensor_scalar(
                    out=u01[:], in0=sums[:, 0:1], scalar1=1.0 - H / CH,
                    scalar2=sums[:, 1:2], op0=ALU.mult, op1=ALU.add,
                )
                nc.vector.tensor_tensor(
                    out=inv_hn[:], in0=rstd_hn[:], in1=rstd_hn[:], op=ALU.mult
                )
                nc.vector.tensor_scalar_mul(
                    out=dsc[:], in0=rstd_hn[:], scalar1=g_xn["inv_n"]
                )
                nc.vector.tensor_scalar_mul(
                    out=negfac[:], in0=inv_hn[:], scalar1=-g_xn["inv_n"]
                )
            if k == 3:
                nc.vector.tensor_scalar(
                    out=g_xn["totp"][:], in0=sums[:, 2:3], scalar1=u01[:, 0:1],
                    scalar2=sums[:, 3:4], op0=ALU.add, op1=ALU.add,
                )
        square(g_xn, 3, yxn[:, 1536:2048], 512)
        nc.vector.tensor_scalar(
            out=e01[:], in0=sq[:, 0:1], scalar1=H * EPS,
            scalar2=sq[:, 1:2], op0=ALU.add, op1=ALU.add,
        )
        stats_dm(g_xn, dms[:], dsc[:, 0:1])
        nc.vector.tensor_scalar(
            out=g_xn["aa"][:], in0=sq[:, 2:3], scalar1=e01[:, 0:1],
            scalar2=negfac[:, 0:1], op0=ALU.add, op1=ALU.mult,
        )
        stats_kk(g_xn, dms[:, 0:1])
        stats_rsqrt(g_xn, negfac[:, 0:1])
        rho = g_xn["rstd"]
        stats_dm(g_xn, g_xn["dm"][:], g_xn["inv_n"])
        stats_negmean(g_xn)
        nb = col("xn_nb")

        def p1(j):
            cc, n = chunks[j]
            nc.vector.scalar_tensor_tensor(
                out=yxn[:, cc : cc + n], in0=yxn[:, cc : cc + n], scalar=rho[:, 0:1],
                in1=qn[:, cc : cc + n], op0=ALU.mult, op1=ALU.add,
            )

        def p2(j):
            cc, n = chunks[j]
            nc.scalar.activation(
                out=yxn[:, cc : cc + n], in_=yxn[:, cc : cc + n], func=ACT.Tanh,
                bias=nb[:, 0:1], scale=rstd_hn[:, 0:1],
            )

        def p3(j):
            cc, n = chunks[j]
            sl = yxn[:, cc : cc + n]
            nc.vector.tensor_tensor(out=sl, in0=sl, in1=omz[:, cc : cc + n], op=ALU.mult)

        def p4(j):
            cc, n = chunks[j]
            sl = yxn[:, cc : cc + n]
            nc.vector.tensor_tensor(out=sl, in0=sl, in1=zh[:, cc : cc + n], op=ALU.subtract)
            nc.sync.dma_start(out=out[:, cc : cc + n], in_=sl)

        p1(0)
        nc.vector.tensor_scalar(
            out=nb[:], in0=g_xn["negmean"][:], scalar1=rho[:, 0:1], scalar2=rstd_hn[:, 0:1],
            op0=ALU.mult, op1=ALU.mult,
        )
        p2(0)
        p1(1)
        p2(1)
        p1(2)
        p2(2)
        p1(3)
        p2(3)
        p1(4)
        p2(4)
        p3(0)
        p3(1)
        p4(0)
        p3(2)
        p4(1)
        p3(3)
        p4(2)
        p3(4)
        p4(3)
        p4(4)
